import numpy as np
import ml_dtypes


def mxq(x, axis, fmt="e4m3"):
    dtype, down = {"e4m3": (ml_dtypes.float8_e4m3fn, 7), "e5m2": (ml_dtypes.float8_e5m2, 14)}[fmt]
    v = np.moveaxis(np.asarray(x, np.float32).astype(ml_dtypes.bfloat16).astype(np.float64), axis, -1)
    blocks = v.reshape(v.shape[:-1] + (-1, 32))
    amax = np.abs(blocks).max(-1, keepdims=True)
    byte = np.maximum(np.where(amax > 0, np.frexp(amax)[1] - 1 + 127, 0) - down, 1)
    scale = np.exp2(byte - 127.0)
    codes = (blocks / scale).astype(np.float32).astype(dtype).astype(np.float64)
    return np.moveaxis((codes * scale).reshape(v.shape), -1, axis)


WIDE = False


def mx_kscale(k):
    if not WIDE:
        return np.ones(k)
    levels = np.array([10, -10, 5, -5, 0])
    a = np.random.permutation(np.resize(levels, k // 512 * 4)).reshape(k // 512, 4)
    idx = np.arange(k)
    return np.exp2(a[idx // 512, idx % 128 // 32])


BF16 = ml_dtypes.bfloat16


def bf(x):
    return np.asarray(x, np.float32).astype(BF16)


def f64(x):
    return np.asarray(x).astype(np.float64)


B, N, D = 128, 17, 1024
LN_EPS = 1e-5
LEAKY_SLOPE = 0.01


def setup_inputs():
    s = mx_kscale(D)
    s = s / s.max()
    return {"h": bf(np.random.standard_normal((B, N, D)) * 0.5 * s),
            "W_l": bf(np.random.standard_normal((D, D)) * 2.0 / np.sqrt(D) / s[None, :]),
            "b_l": bf(np.random.standard_normal(D) * 0.1),
            "W_r": bf(np.random.standard_normal((D, D)) * 1.0 / np.sqrt(D) / s[None, :]),
            "ln_g": bf(1.0 + 0.1 * np.random.standard_normal(D)),
            "ln_b": bf(-0.4 + 0.2 * np.random.standard_normal(D))}


def reference(h, W_l, b_l, W_r, ln_g, ln_b):
    h = f64(h)
    n = h.shape[1]
    mean_neigh = (np.sum(h, axis=1, keepdims=True) - h) / (n - 1)
    c = ((mxq(mean_neigh, 2, "e4m3") @ mxq(f64(W_l), 1, "e4m3").T) + f64(b_l)
         + (mxq(h, 2, "e4m3") @ mxq(f64(W_r), 1, "e4m3").T))
    mu = np.mean(c, axis=-1, keepdims=True)
    var = np.mean(np.square(c - mu), axis=-1, keepdims=True)
    y = (c - mu) * (1.0 / np.sqrt(var + LN_EPS)) * f64(ln_g) + f64(ln_b)
    a = np.where(y > 0, y, LEAKY_SLOPE * y)
    return a + h

@@ -1,0 +1,275 @@
+from contextlib import ExitStack
+
+import concourse.mybir as mybir
+from concourse.masks import make_identity
+
+F32 = mybir.dt.float32
+BF16 = mybir.dt.bfloat16
+U32 = mybir.dt.uint32
+U8 = mybir.dt.uint8
+FP8X4 = mybir.dt.float8_e4m3fn_x4
+ALU = mybir.AluOpType
+ACT = mybir.ActivationFunctionType
+
+P = 128
+GRAPHS = 128
+NODES = 17
+ROWS = GRAPHS * NODES
+D = 1024
+PACK = 4
+K_PASS = P * PACK
+PASSES = D // K_PASS
+BANK = 512
+HALVES = D // BANK
+ROW_TILES = ROWS // P
+W_TILES = D // P
+W_TILES_PER_LOAD = 2
+SRC_GRAPHS = P // NODES
+SRC_ROWS = SRC_GRAPHS * NODES
+SOURCES = -(-ROWS // SRC_ROWS)
+AHEAD = 2
+LN_EPS = 1e-5
+LEAKY_SLOPE = 0.01
+
+FLOPS = 2 * 2 * ROWS * D * D
+
+
+def tile_gnnnicheencoder_pa_kernel(tc, h, W_l, b_l, W_r, ln_g, ln_b, out):
+    nc = tc.nc
+    h_rows = h.flatten_outer_dims()
+    out_rows = out.flatten_outer_dims()
+
+    with ExitStack() as stack:
+        consts = stack.enter_context(tc.tile_pool(name="consts", bufs=1))
+        keep = stack.enter_context(tc.tile_pool(name="keep", bufs=1))
+        src_pool = stack.enter_context(tc.tile_pool(name="src", bufs=5))
+        turn_psum = stack.enter_context(tc.psum_pool(name="turn_psum", bufs=4))
+        acc_psum = stack.enter_context(tc.psum_pool(name="acc_psum", bufs=4))
+
+        eps = consts.tile([P, 1], F32)
+        nc.vector.memset(eps[:], LN_EPS)
+        warm = consts.tile([P, 1], F32)
+        nc.scalar.activation(out=warm[:], in_=eps[:], func=ACT.Sqrt)
+
+        ident = consts.tile([P, P], F32)
+        make_identity(nc, ident[:])
+
+        neigh_f32 = consts.tile([P, P], F32)
+        nc.gpsimd.memset(neigh_f32[:], 0.0)
+        nc.gpsimd.memset(neigh_f32[:, 0:SRC_ROWS], 1.0 / (NODES - 1))
+        by_graph = neigh_f32[:, 0:SRC_ROWS].rearrange("p (c j) -> p c j", j=NODES)
+        nc.gpsimd.affine_select(
+            out=by_graph, in_=by_graph, compare_op=ALU.is_ge, fill=0.0,
+            base=0, pattern=[[-NODES, SRC_GRAPHS], [0, NODES]], channel_multiplier=1,
+        )
+        nc.gpsimd.affine_select(
+            out=by_graph, in_=by_graph, compare_op=ALU.is_ge, fill=0.0,
+            base=NODES - 1, pattern=[[NODES, SRC_GRAPHS], [0, NODES]], channel_multiplier=-1,
+        )
+        nc.gpsimd.affine_select(
+            out=neigh_f32[:], in_=neigh_f32[:], compare_op=ALU.not_equal, fill=0.0,
+            base=0, pattern=[[-1, P]], channel_multiplier=1,
+        )
+        neigh = consts.tile([P, P], BF16)
+        nc.vector.tensor_copy(out=neigh[:], in_=neigh_f32[:])
+
+        ones = consts.tile([P, P], BF16)
+        nc.vector.memset(ones[:], 1.0)
+        vec_rows = consts.tile([P, 3, D], BF16)
+        nc.vector.memset(vec_rows[:], 0.0)
+        for j, vec in enumerate((b_l, ln_g, ln_b)):
+            nc.scalar.dma_start(out=vec_rows[0:1, j, :], in_=vec.unsqueeze(0))
+        spread = consts.tile([P, 3, D], F32)
+        bias_all, gain_all, shift_all = spread[:, 0, :], spread[:, 1, :], spread[:, 2, :]
+
+        def grouped_tiles(pool, name, width):
+            return [pool.tile([P, width, PACK], BF16, name="%s_grouped%d" % (name, g), align_bytes=64)
+                    for g in range(PASSES)]
+
+        def quantised_tiles(name, width):
+            codes = [keep.tile([P, width], U32, name="%s_codes%d" % (name, g), align_bytes=64)
+                     for g in range(PASSES)]
+            scales = [keep.tile([P, width], U8, name="%s_scales%d" % (name, g), align_bytes=64)
+                      for g in range(PASSES)]
+            return codes, scales
+
+        h_grouped = grouped_tiles(keep, "h", ROWS)
+        m_grouped = grouped_tiles(keep, "m", ROWS)
+        h_codes, h_scales = quantised_tiles("h", ROWS)
+        m_codes, m_scales = quantised_tiles("m", ROWS)
+        wl_codes, wl_scales = quantised_tiles("wl", D)
+        wr_codes, wr_scales = quantised_tiles("wr", D)
+
+        def quantise(grouped, codes, scales, first, count):
+            nc.vector.quantize_mx(
+                out=codes[:, first:first + count].bitcast(FP8X4),
+                scales=scales[:, first:first + count],
+                in_=grouped[:, first:first + count, :].rearrange("p c t -> p (c t)"),
+            )
+
+        with tc.tile_pool(name="w_stage", bufs=1) as w_stage:
+            weights = (("wl", W_l, wl_codes, wl_scales), ("wr", W_r, wr_codes, wr_scales))
+            w_nat = {}
+            w_grouped = {}
+            for name, w, codes, scales in weights:
+                w_nat[name] = w_stage.tile([P, W_TILES, D], BF16, name="%s_nat" % name)
+                w_grouped[name] = grouped_tiles(w_stage, name, D)
+            tiles_per_half = W_TILES // HALVES
+            for half in range(HALVES):
+                for name, w, codes, scales in weights:
+                    for ot in range(half * tiles_per_half, (half + 1) * tiles_per_half, W_TILES_PER_LOAD):
+                        some = slice(ot, ot + W_TILES_PER_LOAD)
+                        nc.sync.dma_start(
+                            out=w_nat[name][:, some, :],
+                            in_=w.rearrange("(t p) k -> p t k", p=P)[:, some, :],
+                        )
+
+            for half in range(HALVES):
+                for name, w, codes, scales in weights:
+                    for ot in range(half * tiles_per_half, (half + 1) * tiles_per_half):
+                        words = w_nat[name][:, ot, :].bitcast(F32)
+                        turned = turn_psum.tile([P, PACK, P], F32, tag="turn")
+                        for gu in range(PACK):
+                            nc.tensor.transpose(turned[:, gu, :], words[:, gu * P:(gu + 1) * P], ident[:])
+                        for g in range(PASSES):
+                            dst = w_grouped[name][g][:].bitcast(F32)[:, ot * P:(ot + 1) * P, :]
+                            src = turned[:, 2 * g:2 * g + 2, :].rearrange("p u o -> p o u")
+                            if ot % 2 == 0:
+                                nc.scalar.copy(out=dst, in_=src)
+                            else:
+                                nc.vector.tensor_copy(out=dst, in_=src)
+                    for g in range(PASSES):
+                        quantise(w_grouped[name][g], codes[g], scales[g], half * BANK, BANK)
+
+        for j in range(3):
+            for half in range(HALVES):
+                cols = slice(half * BANK, (half + 1) * BANK)
+                rep = turn_psum.tile([P, BANK], F32, tag="turn")
+                nc.tensor.matmul(rep[:], lhsT=ones[:], rhs=vec_rows[:, j, cols], start=True, stop=True)
+                nc.scalar.copy(out=spread[:, j, cols], in_=rep[:])
+
+        work = stack.enter_context(tc.tile_pool(name="work", bufs=3))
+        stats = stack.enter_context(tc.tile_pool(name="stats", bufs=4))
+
+        def prepare_source(s):
+            first = s * SRC_ROWS
+            fresh = min(SRC_ROWS, ROWS - first)
+            loaded = min(P, ROWS - first)
+            src = src_pool.tile([P, D], BF16)
+            if loaded < P:
+                nc.gpsimd.memset(src[:], 0.0)
+            nc.sync.dma_start(out=src[0:loaded, :], in_=h_rows[first:first + loaded, :])
+
+            words = src[:].bitcast(F32)
+            turned = turn_psum.tile([P, PACK, P], F32, tag="turn")
+            for gu in range(PACK):
+                nc.tensor.transpose(turned[:, gu, :], words[:, gu * P:(gu + 1) * P], ident[:])
+            for g in range(PASSES):
+                nc.scalar.copy(
+                    out=h_grouped[g][:].bitcast(F32)[:, first:first + fresh, :],
+                    in_=turned[:, 2 * g:2 * g + 2, 0:fresh].rearrange("p u r -> p r u"),
+                )
+
+            by_value = src[:].rearrange("p (g u q e) -> p g u e q", g=PASSES, u=2, e=2)
+            for g in range(PASSES):
+                mean = turn_psum.tile([P, PACK, P], F32, tag="turn")
+                for u in range(2):
+                    for e in range(2):
+                        nc.tensor.matmul(mean[:, 2 * u + e, :], lhsT=by_value[:, g, u, e, :], rhs=neigh[:],
+                                         start=True, stop=True)
+                nc.scalar.copy(
+                    out=m_grouped[g][:, first:first + fresh, :],
+                    in_=mean[:, :, 0:fresh].rearrange("p t r -> p r t"),
+                )
+
+        def sources_for_rows_below(row):
+            return -(-row // SRC_ROWS)
+
+        def prepare_rows(t):
+            for s in range(sources_for_rows_below(t * P), sources_for_rows_below((t + 1) * P)):
+                prepare_source(s)
+            for g in range(PASSES):
+                quantise(h_grouped[g], h_codes[g], h_scales[g], t * P, P)
+                quantise(m_grouped[g], m_codes[g], m_scales[g], t * P, P)
+
+        def multiply(t):
+            rows = slice(t * P, (t + 1) * P)
+            products = []
+            for g in range(PASSES):
+                products.append((m_codes[g], m_scales[g], wl_codes[g], wl_scales[g]))
+                products.append((h_codes[g], h_scales[g], wr_codes[g], wr_scales[g]))
+            accs = []
+            for half in range(HALVES):
+                cols = slice(half * BANK, (half + 1) * BANK)
+                acc = acc_psum.tile([P, BANK], F32, tag="acc")
+                for i, (x_codes, x_scales, w_codes, w_scales) in enumerate(products):
+                    nc.tensor.matmul_mx(
+                        out=acc[:],
+                        lhsT=x_codes[:, rows].bitcast(FP8X4),
+                        lhsT_scale=x_scales[:, rows],
+                        rhs=w_codes[:, cols].bitcast(FP8X4),
+                        rhs_scale=w_scales[:, cols],
+                        start=(i == 0),
+                        stop=(i == len(products) - 1),
+                    )
+                accs.append(acc)
+            return accs
+
+        def centre(t, accs):
+            c = work.tile([P, D], F32, tag="c")
+            c_sum = stats.tile([P, HALVES], F32, tag="c_sum")
+            for half in range(HALVES):
+                cols = slice(half * BANK, (half + 1) * BANK)
+                nc.vector.scalar_tensor_tensor(
+                    out=c[:, cols], in0=accs[half][:], scalar=1.0, in1=bias_all[:, cols],
+                    op0=ALU.mult, op1=ALU.add, accum_out=c_sum[:, half:half + 1],
+                )
+            neg_mean = stats.tile([P, 1], F32, tag="neg_mean")
+            nc.vector.tensor_scalar(
+                out=neg_mean[:], in0=c_sum[:, 0:1], scalar1=c_sum[:, 1:2], scalar2=-1.0 / D,
+                op0=ALU.add, op1=ALU.mult,
+            )
+            squares = work.tile([P, D], BF16, tag="squares")
+            sq_sum = stats.tile([P, 1], F32, tag="sq_sum")
+            nc.scalar.activation(out=squares[:], in_=c[:], func=ACT.Square, bias=neg_mean[:, 0:1],
+                                 scale=1.0, accum_out=sq_sum[:])
+            std = stats.tile([P, 1], F32, tag="std")
+            nc.scalar.activation(out=std[:], in_=sq_sum[:], func=ACT.Sqrt, bias=eps[:, 0:1], scale=1.0 / D)
+            y = work.tile([P, D], F32, tag="y")
+            for half in range(HALVES):
+                cols = slice(half * BANK, (half + 1) * BANK)
+                nc.vector.scalar_tensor_tensor(
+                    out=y[:, cols], in0=c[:, cols], scalar=neg_mean[:, 0:1], in1=gain_all[:, cols],
+                    op0=ALU.add, op1=ALU.mult,
+                )
+            return y, std
+
+        def finish(t, y, std):
+            rows = slice(t * P, (t + 1) * P)
+            h_res = work.tile([P, D], BF16, tag="h_res")
+            nc.sync.dma_start(out=h_res[:], in_=h_rows[rows, :])
+            rstd = stats.tile([P, 1], F32, tag="rstd")
+            nc.vector.reciprocal(out=rstd[:], in_=std[:])
+            halves = [slice(half * BANK, (half + 1) * BANK) for half in range(HALVES)]
+            for cols in halves:
+                nc.vector.scalar_tensor_tensor(
+                    out=y[:, cols], in0=y[:, cols], scalar=rstd[:, 0:1], in1=shift_all[:, cols],
+                    op0=ALU.mult, op1=ALU.add,
+                )
+            for cols in halves:
+                nc.vector.scalar_tensor_tensor(
+                    out=y[:, cols], in0=y[:, cols], scalar=LEAKY_SLOPE, in1=y[:, cols],
+                    op0=ALU.mult, op1=ALU.max,
+                )
+            for cols in halves:
+                nc.vector.tensor_tensor(out=y[:, cols], in0=y[:, cols], in1=h_res[:, cols], op=ALU.add)
+            nc.gpsimd.dma_start(out=out_rows[rows, :], in_=y[:])
+
+        for t in range(AHEAD):
+            prepare_rows(t)
+        for t in range(ROW_TILES):
+            accs = multiply(t)
+            y, std = centre(t, accs)
+            if t + AHEAD < ROW_TILES:
+                prepare_rows(t + AHEAD)
+            finish(t, y, std)

@@ -43,8 +43,9 @@ def tile_gnnnicheencoder_pa_kernel(tc, h, W_l, b_l, W_r, ln_g, ln_b, out):
         consts = stack.enter_context(tc.tile_pool(name="consts", bufs=1))
         keep = stack.enter_context(tc.tile_pool(name="keep", bufs=1))
         src_pool = stack.enter_context(tc.tile_pool(name="src", bufs=5))
-        turn_psum = stack.enter_context(tc.psum_pool(name="turn_psum", bufs=4))
-        acc_psum = stack.enter_context(tc.psum_pool(name="acc_psum", bufs=4))
+        const_psum = stack.enter_context(tc.psum_pool(name="const_psum", bufs=1))
+        turn_psum = stack.enter_context(tc.psum_pool(name="turn_psum", bufs=2))
+        acc_psum = stack.enter_context(tc.psum_pool(name="acc_psum", bufs=2))
 
         eps = consts.tile([P, 1], F32)
         nc.vector.memset(eps[:], LN_EPS)
@@ -79,8 +80,7 @@ def tile_gnnnicheencoder_pa_kernel(tc, h, W_l, b_l, W_r, ln_g, ln_b, out):
         nc.vector.memset(vec_rows[:], 0.0)
         for j, vec in enumerate((b_l, ln_g, ln_b)):
             nc.scalar.dma_start(out=vec_rows[0:1, j, :], in_=vec.unsqueeze(0))
-        spread = consts.tile([P, 3, D], F32)
-        bias_all, gain_all, shift_all = spread[:, 0, :], spread[:, 1, :], spread[:, 2, :]
+        bias_all = consts.tile([P, D], F32)
 
         def grouped_tiles(pool, name, width):
             return [pool.tile([P, width, PACK], BF16, name="%s_grouped%d" % (name, g), align_bytes=64)
@@ -141,12 +141,19 @@ def tile_gnnnicheencoder_pa_kernel(tc, h, W_l, b_l, W_r, ln_g, ln_b, out):
                     for g in range(PASSES):
                         quantise(w_grouped[name][g], codes[g], scales[g], half * BANK, BANK)
 
-        for j in range(3):
-            for half in range(HALVES):
-                cols = slice(half * BANK, (half + 1) * BANK)
-                rep = turn_psum.tile([P, BANK], F32, tag="turn")
-                nc.tensor.matmul(rep[:], lhsT=ones[:], rhs=vec_rows[:, j, cols], start=True, stop=True)
-                nc.scalar.copy(out=spread[:, j, cols], in_=rep[:])
+        gain_all = []
+        shift_all = []
+        for half in range(HALVES):
+            cols = slice(half * BANK, (half + 1) * BANK)
+            rep = turn_psum.tile([P, BANK], F32, tag="turn")
+            nc.tensor.matmul(rep[:], lhsT=ones[:], rhs=vec_rows[:, 0, cols], start=True, stop=True)
+            nc.scalar.copy(out=bias_all[:, cols], in_=rep[:])
+            gain = const_psum.tile([P, BANK], F32, name="gain%d" % half)
+            nc.tensor.matmul(gain[:], lhsT=ones[:], rhs=vec_rows[:, 1, cols], start=True, stop=True)
+            gain_all.append(gain)
+            shift = const_psum.tile([P, BANK], F32, name="shift%d" % half)
+            nc.tensor.matmul(shift[:], lhsT=ones[:], rhs=vec_rows[:, 2, cols], start=True, stop=True)
+            shift_all.append(shift)
 
         work = stack.enter_context(tc.tile_pool(name="work", bufs=3))
         stats = stack.enter_context(tc.tile_pool(name="stats", bufs=4))
@@ -235,11 +242,11 @@ def tile_gnnnicheencoder_pa_kernel(tc, h, W_l, b_l, W_r, ln_g, ln_b, out):
                                  scale=1.0, accum_out=sq_sum[:])
             std = stats.tile([P, 1], F32, tag="std")
             nc.scalar.activation(out=std[:], in_=sq_sum[:], func=ACT.Sqrt, bias=eps[:, 0:1], scale=1.0 / D)
-            y = work.tile([P, D], F32, tag="y")
+            y = work.tile([P, D], F32, tag="y", bufs=4)
             for half in range(HALVES):
                 cols = slice(half * BANK, (half + 1) * BANK)
                 nc.vector.scalar_tensor_tensor(
-                    out=y[:, cols], in0=c[:, cols], scalar=neg_mean[:, 0:1], in1=gain_all[:, cols],
+                    out=y[:, cols], in0=c[:, cols], scalar=neg_mean[:, 0:1], in1=gain_all[half][:],
                     op0=ALU.add, op1=ALU.mult,
                 )
             return y, std
@@ -251,9 +258,9 @@ def tile_gnnnicheencoder_pa_kernel(tc, h, W_l, b_l, W_r, ln_g, ln_b, out):
             rstd = stats.tile([P, 1], F32, tag="rstd")
             nc.vector.reciprocal(out=rstd[:], in_=std[:])
             halves = [slice(half * BANK, (half + 1) * BANK) for half in range(HALVES)]
-            for cols in halves:
+            for half, cols in enumerate(halves):
                 nc.vector.scalar_tensor_tensor(
-                    out=y[:, cols], in0=y[:, cols], scalar=rstd[:, 0:1], in1=shift_all[:, cols],
+                    out=y[:, cols], in0=y[:, cols], scalar=rstd[:, 0:1], in1=shift_all[half][:],
                     op0=ALU.mult, op1=ALU.add,
                 )
             for cols in halves:
@@ -261,8 +268,7 @@ def tile_gnnnicheencoder_pa_kernel(tc, h, W_l, b_l, W_r, ln_g, ln_b, out):
                     out=y[:, cols], in0=y[:, cols], scalar=LEAKY_SLOPE, in1=y[:, cols],
                     op0=ALU.mult, op1=ALU.max,
                 )
-            for cols in halves:
-                nc.vector.tensor_tensor(out=y[:, cols], in0=y[:, cols], in1=h_res[:, cols], op=ALU.add)
+            nc.gpsimd.tensor_tensor(out=y[:], in0=y[:], in1=h_res[:], op=ALU.add)
             nc.gpsimd.dma_start(out=out_rows[rows, :], in_=y[:])
 
         for t in range(AHEAD):

@@ -22,12 +22,11 @@ PASSES = D // K_PASS
 BANK = 512
 HALVES = D // BANK
 ROW_TILES = ROWS // P
-W_TILES = D // P
 W_TILES_PER_LOAD = 2
+W_LOADS_PER_HALF = BANK // (P * W_TILES_PER_LOAD)
 SRC_GRAPHS = P // NODES
 SRC_ROWS = SRC_GRAPHS * NODES
-SOURCES = -(-ROWS // SRC_ROWS)
-AHEAD = 2
+LEAD = 2
 LN_EPS = 1e-5
 LEAKY_SLOPE = 0.01
 
@@ -38,19 +37,22 @@ def tile_gnnnicheencoder_pa_kernel(tc, h, W_l, b_l, W_r, ln_g, ln_b, out):
     nc = tc.nc
     h_rows = h.flatten_outer_dims()
     out_rows = out.flatten_outer_dims()
+    halves = [slice(half * BANK, (half + 1) * BANK) for half in range(HALVES)]
 
     with ExitStack() as stack:
         consts = stack.enter_context(tc.tile_pool(name="consts", bufs=1))
         keep = stack.enter_context(tc.tile_pool(name="keep", bufs=1))
+        w_stage = stack.enter_context(tc.tile_pool(name="w_stage", bufs=4))
         src_pool = stack.enter_context(tc.tile_pool(name="src", bufs=5))
-        const_psum = stack.enter_context(tc.psum_pool(name="const_psum", bufs=1))
-        turn_psum = stack.enter_context(tc.psum_pool(name="turn_psum", bufs=2))
-        acc_psum = stack.enter_context(tc.psum_pool(name="acc_psum", bufs=2))
+        work = stack.enter_context(tc.tile_pool(name="work", bufs=3))
+        stats = stack.enter_context(tc.tile_pool(name="stats", bufs=LEAD + 2))
+        turn_psum = stack.enter_context(tc.psum_pool(name="turn_psum", bufs=4))
+        acc_psum = stack.enter_context(tc.psum_pool(name="acc_psum", bufs=4))
 
         eps = consts.tile([P, 1], F32)
         nc.vector.memset(eps[:], LN_EPS)
         warm = consts.tile([P, 1], F32)
-        nc.scalar.activation(out=warm[:], in_=eps[:], func=ACT.Sqrt)
+        nc.scalar.activation(out=warm[:], in_=eps[:], func=ACT.Abs_reciprocal_sqrt)
 
         ident = consts.tile([P, P], F32)
         make_identity(nc, ident[:])
@@ -80,11 +82,15 @@ def tile_gnnnicheencoder_pa_kernel(tc, h, W_l, b_l, W_r, ln_g, ln_b, out):
         nc.vector.memset(vec_rows[:], 0.0)
         for j, vec in enumerate((b_l, ln_g, ln_b)):
             nc.scalar.dma_start(out=vec_rows[0:1, j, :], in_=vec.unsqueeze(0))
-        bias_all = consts.tile([P, D], F32)
+        spread = consts.tile([P, 3, D], BF16)
+        bias_all, gain_all, shift_all = spread[:, 0, :], spread[:, 1, :], spread[:, 2, :]
 
-        def grouped_tiles(pool, name, width):
-            return [pool.tile([P, width, PACK], BF16, name="%s_grouped%d" % (name, g), align_bytes=64)
-                    for g in range(PASSES)]
+        def spread_vectors():
+            for j in range(3):
+                for cols in halves:
+                    rep = turn_psum.tile([P, BANK], F32, tag="turn")
+                    nc.tensor.matmul(rep[:], lhsT=ones[:], rhs=vec_rows[:, j, cols], start=True, stop=True)
+                    nc.scalar.copy(out=spread[:, j, cols], in_=rep[:])
 
         def quantised_tiles(name, width):
             codes = [keep.tile([P, width], U32, name="%s_codes%d" % (name, g), align_bytes=64)
@@ -93,72 +99,45 @@ def tile_gnnnicheencoder_pa_kernel(tc, h, W_l, b_l, W_r, ln_g, ln_b, out):
                       for g in range(PASSES)]
             return codes, scales
 
-        h_grouped = grouped_tiles(keep, "h", ROWS)
-        m_grouped = grouped_tiles(keep, "m", ROWS)
+        h_grouped = [keep.tile([P, ROWS, PACK], BF16, name="h_grouped%d" % g, align_bytes=64)
+                     for g in range(PASSES)]
+        m_grouped = [keep.tile([P, ROWS, PACK], BF16, name="m_grouped%d" % g, align_bytes=64)
+                     for g in range(PASSES)]
         h_codes, h_scales = quantised_tiles("h", ROWS)
         m_codes, m_scales = quantised_tiles("m", ROWS)
         wl_codes, wl_scales = quantised_tiles("wl", D)
         wr_codes, wr_scales = quantised_tiles("wr", D)
 
-        def quantise(grouped, codes, scales, first, count):
+        def quantise(grouped, codes, scales):
             nc.vector.quantize_mx(
-                out=codes[:, first:first + count].bitcast(FP8X4),
-                scales=scales[:, first:first + count],
-                in_=grouped[:, first:first + count, :].rearrange("p c t -> p (c t)"),
-            )
+                out=codes.bitcast(FP8X4), scales=scales, in_=grouped.rearrange("p c t -> p (c t)"))
 
-        with tc.tile_pool(name="w_stage", bufs=1) as w_stage:
-            weights = (("wl", W_l, wl_codes, wl_scales), ("wr", W_r, wr_codes, wr_scales))
-            w_nat = {}
-            w_grouped = {}
-            for name, w, codes, scales in weights:
-                w_nat[name] = w_stage.tile([P, W_TILES, D], BF16, name="%s_nat" % name)
-                w_grouped[name] = grouped_tiles(w_stage, name, D)
-            tiles_per_half = W_TILES // HALVES
-            for half in range(HALVES):
-                for name, w, codes, scales in weights:
-                    for ot in range(half * tiles_per_half, (half + 1) * tiles_per_half, W_TILES_PER_LOAD):
-                        some = slice(ot, ot + W_TILES_PER_LOAD)
-                        nc.sync.dma_start(
-                            out=w_nat[name][:, some, :],
-                            in_=w.rearrange("(t p) k -> p t k", p=P)[:, some, :],
-                        )
-
-            for half in range(HALVES):
-                for name, w, codes, scales in weights:
-                    for ot in range(half * tiles_per_half, (half + 1) * tiles_per_half):
-                        words = w_nat[name][:, ot, :].bitcast(F32)
+        def prepare_weights(half):
+            for w, codes, scales in ((W_l, wl_codes, wl_scales), (W_r, wr_codes, wr_scales)):
+                by_tile = w.rearrange("(t p) k -> p t k", p=P)
+                w_grouped = [w_stage.tile([P, BANK, PACK], BF16, name="w_grouped%d" % g, tag="w_grouped",
+                                          align_bytes=64) for g in range(PASSES)]
+                for load in range(W_LOADS_PER_HALF):
+                    first_tile = (half * W_LOADS_PER_HALF + load) * W_TILES_PER_LOAD
+                    w_nat = w_stage.tile([P, W_TILES_PER_LOAD, D], BF16, tag="w_nat")
+                    nc.sync.dma_start(out=w_nat[:], in_=by_tile[:, first_tile:first_tile + W_TILES_PER_LOAD, :])
+                    for i in range(W_TILES_PER_LOAD):
+                        words = w_nat[:, i, :].bitcast(F32)
                         turned = turn_psum.tile([P, PACK, P], F32, tag="turn")
                         for gu in range(PACK):
                             nc.tensor.transpose(turned[:, gu, :], words[:, gu * P:(gu + 1) * P], ident[:])
+                        first_col = (load * W_TILES_PER_LOAD + i) * P
                         for g in range(PASSES):
-                            dst = w_grouped[name][g][:].bitcast(F32)[:, ot * P:(ot + 1) * P, :]
-                            src = turned[:, 2 * g:2 * g + 2, :].rearrange("p u o -> p o u")
-                            if ot % 2 == 0:
-                                nc.scalar.copy(out=dst, in_=src)
+                            dst = w_grouped[g][:].bitcast(F32)[:, first_col:first_col + P, :]
+                            pairs = turned[:, 2 * g:2 * g + 2, :].rearrange("p u o -> p o u")
+                            if i % 2 == 0:
+                                nc.scalar.copy(out=dst, in_=pairs)
                             else:
-                                nc.vector.tensor_copy(out=dst, in_=src)
-                    for g in range(PASSES):
-                        quantise(w_grouped[name][g], codes[g], scales[g], half * BANK, BANK)
+                                nc.vector.tensor_copy(out=dst, in_=pairs)
+                for g in range(PASSES):
+                    quantise(w_grouped[g][:], codes[g][:, halves[half]], scales[g][:, halves[half]])
 
-        gain_all = []
-        shift_all = []
-        for half in range(HALVES):
-            cols = slice(half * BANK, (half + 1) * BANK)
-            rep = turn_psum.tile([P, BANK], F32, tag="turn")
-            nc.tensor.matmul(rep[:], lhsT=ones[:], rhs=vec_rows[:, 0, cols], start=True, stop=True)
-            nc.scalar.copy(out=bias_all[:, cols], in_=rep[:])
-            gain = const_psum.tile([P, BANK], F32, name="gain%d" % half)
-            nc.tensor.matmul(gain[:], lhsT=ones[:], rhs=vec_rows[:, 1, cols], start=True, stop=True)
-            gain_all.append(gain)
-            shift = const_psum.tile([P, BANK], F32, name="shift%d" % half)
-            nc.tensor.matmul(shift[:], lhsT=ones[:], rhs=vec_rows[:, 2, cols], start=True, stop=True)
-            shift_all.append(shift)
-
-        work = stack.enter_context(tc.tile_pool(name="work", bufs=3))
-        stats = stack.enter_context(tc.tile_pool(name="stats", bufs=4))
-
-        def prepare_source(s):
+        def turn_source(s):
             first = s * SRC_ROWS
             fresh = min(SRC_ROWS, ROWS - first)
             loaded = min(P, ROWS - first)
@@ -192,90 +171,123 @@ def tile_gnnnicheencoder_pa_kernel(tc, h, W_l, b_l, W_r, ln_g, ln_b, out):
         def sources_for_rows_below(row):
             return -(-row // SRC_ROWS)
 
-        def prepare_rows(t):
+        def turn_rows(t):
             for s in range(sources_for_rows_below(t * P), sources_for_rows_below((t + 1) * P)):
-                prepare_source(s)
-            for g in range(PASSES):
-                quantise(h_grouped[g], h_codes[g], h_scales[g], t * P, P)
-                quantise(m_grouped[g], m_codes[g], m_scales[g], t * P, P)
+                turn_source(s)
 
-        def multiply(t):
+        def quantise_rows(t):
+            rows = slice(t * P, (t + 1) * P)
+            for g in range(PASSES):
+                quantise(h_grouped[g][:, rows, :], h_codes[g][:, rows], h_scales[g][:, rows])
+                quantise(m_grouped[g][:, rows, :], m_codes[g][:, rows], m_scales[g][:, rows])
+
+        def multiply(t, half):
             rows = slice(t * P, (t + 1) * P)
             products = []
             for g in range(PASSES):
                 products.append((m_codes[g], m_scales[g], wl_codes[g], wl_scales[g]))
                 products.append((h_codes[g], h_scales[g], wr_codes[g], wr_scales[g]))
-            accs = []
-            for half in range(HALVES):
-                cols = slice(half * BANK, (half + 1) * BANK)
-                acc = acc_psum.tile([P, BANK], F32, tag="acc")
-                for i, (x_codes, x_scales, w_codes, w_scales) in enumerate(products):
-                    nc.tensor.matmul_mx(
-                        out=acc[:],
-                        lhsT=x_codes[:, rows].bitcast(FP8X4),
-                        lhsT_scale=x_scales[:, rows],
-                        rhs=w_codes[:, cols].bitcast(FP8X4),
-                        rhs_scale=w_scales[:, cols],
-                        start=(i == 0),
-                        stop=(i == len(products) - 1),
-                    )
-                accs.append(acc)
-            return accs
-
-        def centre(t, accs):
-            c = work.tile([P, D], F32, tag="c")
-            c_sum = stats.tile([P, HALVES], F32, tag="c_sum")
-            for half in range(HALVES):
-                cols = slice(half * BANK, (half + 1) * BANK)
-                nc.vector.scalar_tensor_tensor(
-                    out=c[:, cols], in0=accs[half][:], scalar=1.0, in1=bias_all[:, cols],
-                    op0=ALU.mult, op1=ALU.add, accum_out=c_sum[:, half:half + 1],
+            acc = acc_psum.tile([P, BANK], F32, tag="acc")
+            for i, (x_codes, x_scales, w_codes, w_scales) in enumerate(products):
+                nc.tensor.matmul_mx(
+                    out=acc[:],
+                    lhsT=x_codes[:, rows].bitcast(FP8X4),
+                    lhsT_scale=x_scales[:, rows],
+                    rhs=w_codes[:, halves[half]].bitcast(FP8X4),
+                    rhs_scale=w_scales[:, halves[half]],
+                    start=(i == 0),
+                    stop=(i == len(products) - 1),
                 )
-            neg_mean = stats.tile([P, 1], F32, tag="neg_mean")
-            nc.vector.tensor_scalar(
-                out=neg_mean[:], in0=c_sum[:, 0:1], scalar1=c_sum[:, 1:2], scalar2=-1.0 / D,
+            return acc
+
+        c_tiles = {}
+        c_sums = {}
+        neg_means = {}
+        rstds = {}
+        y_tiles = {}
+        h_tiles = {}
+
+        def add_bias(t, half, acc):
+            if half == 0:
+                c_tiles[t] = work.tile([P, D], F32, name="c", tag="c", bufs=LEAD + 2)
+                c_sums[t] = stats.tile([P, HALVES], F32, name="c_sum", tag="c_sum")
+            nc.vector.scalar_tensor_tensor(
+                out=c_tiles[t][:, halves[half]], in0=acc[:], scalar=1.0, in1=bias_all[:, halves[half]],
+                op0=ALU.mult, op1=ALU.add, accum_out=c_sums[t][:, half:half + 1],
+            )
+
+        def statistics(t):
+            scaled = stats.tile([P, HALVES], F32, tag="scaled")
+            neg_means[t] = stats.tile([P, 1], F32, name="neg_mean", tag="neg_mean")
+            nc.scalar.activation(out=scaled[:], in_=c_sums[t][:], func=ACT.Identity, scale=-1.0 / D,
+                                 accum_out=neg_means[t][:])
+            squares = work.tile([P, D], BF16, tag="squares", bufs=2)
+            sq_sum = stats.tile([P, 1], F32, tag="sq_sum")
+            nc.scalar.activation(out=squares[:], in_=c_tiles[t][:], func=ACT.Square, bias=neg_means[t][:, 0:1],
+                                 scale=1.0, accum_out=sq_sum[:])
+            rstds[t] = stats.tile([P, 1], F32, name="rstd", tag="rstd")
+            nc.scalar.activation(out=rstds[t][:], in_=sq_sum[:], func=ACT.Abs_reciprocal_sqrt, bias=eps[:, 0:1],
+                                 scale=1.0 / D)
+
+        def centre_and_gain(t):
+            y_tiles[t] = work.tile([P, D], F32, name="y", tag="y")
+            nc.vector.scalar_tensor_tensor(
+                out=y_tiles[t][:], in0=c_tiles[t][:], scalar=neg_means[t][:, 0:1], in1=gain_all,
                 op0=ALU.add, op1=ALU.mult,
             )
-            squares = work.tile([P, D], BF16, tag="squares")
-            sq_sum = stats.tile([P, 1], F32, tag="sq_sum")
-            nc.scalar.activation(out=squares[:], in_=c[:], func=ACT.Square, bias=neg_mean[:, 0:1],
-                                 scale=1.0, accum_out=sq_sum[:])
-            std = stats.tile([P, 1], F32, tag="std")
-            nc.scalar.activation(out=std[:], in_=sq_sum[:], func=ACT.Sqrt, bias=eps[:, 0:1], scale=1.0 / D)
-            y = work.tile([P, D], F32, tag="y", bufs=4)
-            for half in range(HALVES):
-                cols = slice(half * BANK, (half + 1) * BANK)
-                nc.vector.scalar_tensor_tensor(
-                    out=y[:, cols], in0=c[:, cols], scalar=neg_mean[:, 0:1], in1=gain_all[half][:],
-                    op0=ALU.add, op1=ALU.mult,
-                )
-            return y, std
 
-        def finish(t, y, std):
-            rows = slice(t * P, (t + 1) * P)
-            h_res = work.tile([P, D], BF16, tag="h_res")
-            nc.sync.dma_start(out=h_res[:], in_=h_rows[rows, :])
-            rstd = stats.tile([P, 1], F32, tag="rstd")
-            nc.vector.reciprocal(out=rstd[:], in_=std[:])
-            halves = [slice(half * BANK, (half + 1) * BANK) for half in range(HALVES)]
-            for half, cols in enumerate(halves):
-                nc.vector.scalar_tensor_tensor(
-                    out=y[:, cols], in0=y[:, cols], scalar=rstd[:, 0:1], in1=shift_all[half][:],
-                    op0=ALU.mult, op1=ALU.add,
-                )
-            for cols in halves:
-                nc.vector.scalar_tensor_tensor(
-                    out=y[:, cols], in0=y[:, cols], scalar=LEAKY_SLOPE, in1=y[:, cols],
-                    op0=ALU.mult, op1=ALU.max,
-                )
-            nc.gpsimd.tensor_tensor(out=y[:], in0=y[:], in1=h_res[:], op=ALU.add)
-            nc.gpsimd.dma_start(out=out_rows[rows, :], in_=y[:])
+        def scale_and_shift(t):
+            nc.vector.scalar_tensor_tensor(
+                out=y_tiles[t][:], in0=y_tiles[t][:], scalar=rstds[t][:, 0:1], in1=shift_all,
+                op0=ALU.mult, op1=ALU.add,
+            )
 
-        for t in range(AHEAD):
-            prepare_rows(t)
-        for t in range(ROW_TILES):
-            accs = multiply(t)
-            y, std = centre(t, accs)
-            if t + AHEAD < ROW_TILES:
-                prepare_rows(t + AHEAD)
-            finish(t, y, std)
+        def leaky_relu(t):
+            nc.vector.scalar_tensor_tensor(
+                out=y_tiles[t][:], in0=y_tiles[t][:], scalar=LEAKY_SLOPE, in1=y_tiles[t][:],
+                op0=ALU.mult, op1=ALU.max,
+            )
+
+        def load_residual(t):
+            h_tiles[t] = work.tile([P, D], BF16, name="h_res", tag="h_res")
+            nc.sync.dma_start(out=h_tiles[t][:], in_=h_rows[t * P:(t + 1) * P, :])
+
+        def add_residual_and_store(t):
+            nc.vector.tensor_tensor(out=y_tiles[t][:], in0=y_tiles[t][:], in1=h_tiles[t][:], op=ALU.add)
+            nc.gpsimd.dma_start(out=out_rows[t * P:(t + 1) * P, :], in_=y_tiles[t][:])
+
+        def is_tile(t):
+            return 0 <= t < ROW_TILES
+
+        prepare_weights(0)
+        for t in range(LEAD + 1):
+            turn_rows(t)
+        spread_vectors()
+        for t in range(LEAD):
+            quantise_rows(t)
+            add_bias(t, 0, multiply(t, 0))
+        quantise_rows(LEAD)
+        prepare_weights(1)
+        turn_rows(LEAD + 1)
+        load_residual(0)
+
+        for t in range(ROW_TILES + 1):
+            if is_tile(t):
+                add_bias(t, 1, multiply(t, 1))
+                statistics(t)
+            if is_tile(t - 1):
+                scale_and_shift(t - 1)
+            if is_tile(t + LEAD):
+                add_bias(t + LEAD, 0, multiply(t + LEAD, 0))
+            if is_tile(t - 1):
+                leaky_relu(t - 1)
+            if is_tile(t + LEAD + 1):
+                quantise_rows(t + LEAD + 1)
+            if is_tile(t - 1):
+                add_residual_and_store(t - 1)
+            if is_tile(t):
+                centre_and_gain(t)
+            if is_tile(t + LEAD + 2):
+                turn_rows(t + LEAD + 2)
+            if is_tile(t + 1):
+                load_residual(t + 1)

@@ -254,7 +254,7 @@ def tile_gnnnicheencoder_pa_kernel(tc, h, W_l, b_l, W_r, ln_g, ln_b, out):
 
         def add_residual_and_store(t):
             nc.vector.tensor_tensor(out=y_tiles[t][:], in0=y_tiles[t][:], in1=h_tiles[t][:], op=ALU.add)
-            nc.gpsimd.dma_start(out=out_rows[t * P:(t + 1) * P, :], in_=y_tiles[t][:])
+            nc.sync.dma_start(out=out_rows[t * P:(t + 1) * P, :], in_=y_tiles[t][:])
 
         def is_tile(t):
             return 0 <= t < ROW_TILES

@@ -27,6 +27,10 @@ W_LOADS_PER_HALF = BANK // (P * W_TILES_PER_LOAD)
 SRC_GRAPHS = P // NODES
 SRC_ROWS = SRC_GRAPHS * NODES
 LEAD = 2
+FEATURE_TILES = D // P
+TILES_PER_BANK = BANK // P
+RING_TILES = 5
+RING_ROWS = RING_TILES * P
 LN_EPS = 1e-5
 LEAKY_SLOPE = 0.01
 
@@ -45,9 +49,9 @@ def tile_gnnnicheencoder_pa_kernel(tc, h, W_l, b_l, W_r, ln_g, ln_b, out):
         w_stage = stack.enter_context(tc.tile_pool(name="w_stage", bufs=4))
         src_pool = stack.enter_context(tc.tile_pool(name="src", bufs=5))
         work = stack.enter_context(tc.tile_pool(name="work", bufs=3))
-        stats = stack.enter_context(tc.tile_pool(name="stats", bufs=LEAD + 2))
-        turn_psum = stack.enter_context(tc.psum_pool(name="turn_psum", bufs=4))
-        acc_psum = stack.enter_context(tc.psum_pool(name="acc_psum", bufs=4))
+        stats = stack.enter_context(tc.tile_pool(name="stats", bufs=LEAD + 3))
+        turn_psum = stack.enter_context(tc.psum_pool(name="turn_psum", bufs=6))
+        acc_psum = stack.enter_context(tc.psum_pool(name="acc_psum", bufs=2))
 
         eps = consts.tile([P, 1], F32)
         nc.vector.memset(eps[:], LN_EPS)
@@ -78,19 +82,27 @@ def tile_gnnnicheencoder_pa_kernel(tc, h, W_l, b_l, W_r, ln_g, ln_b, out):
 
         ones = consts.tile([P, P], BF16)
         nc.vector.memset(ones[:], 1.0)
-        vec_rows = consts.tile([P, 3, D], BF16)
+        vec_rows = consts.tile([P, D], BF16)
         nc.vector.memset(vec_rows[:], 0.0)
-        for j, vec in enumerate((b_l, ln_g, ln_b)):
-            nc.scalar.dma_start(out=vec_rows[0:1, j, :], in_=vec.unsqueeze(0))
-        spread = consts.tile([P, 3, D], BF16)
-        bias_all, gain_all, shift_all = spread[:, 0, :], spread[:, 1, :], spread[:, 2, :]
+        nc.scalar.dma_start(out=vec_rows[0:1, :], in_=b_l.unsqueeze(0))
+        bias_all = consts.tile([P, D], BF16)
+        gb_rows = consts.tile([P, P], BF16)
+        nc.vector.memset(gb_rows[:], 0.0)
+        nc.scalar.dma_start(out=gb_rows[0:FEATURE_TILES, :], in_=ln_g.rearrange("(j p) -> j p", p=P))
+        nc.scalar.dma_start(out=gb_rows[FEATURE_TILES:2 * FEATURE_TILES, :], in_=ln_b.rearrange("(j p) -> j p", p=P))
+        gb_rows_f32 = consts.tile([P, P], F32)
+        gb_cols = consts.tile([P, 2 * FEATURE_TILES], F32)
+        gain_col, shift_col = gb_cols[:, 0:FEATURE_TILES], gb_cols[:, FEATURE_TILES:2 * FEATURE_TILES]
 
         def spread_vectors():
-            for j in range(3):
-                for cols in halves:
-                    rep = turn_psum.tile([P, BANK], F32, tag="turn")
-                    nc.tensor.matmul(rep[:], lhsT=ones[:], rhs=vec_rows[:, j, cols], start=True, stop=True)
-                    nc.scalar.copy(out=spread[:, j, cols], in_=rep[:])
+            for cols in halves:
+                rep = turn_psum.tile([P, BANK], F32, tag="turn")
+                nc.tensor.matmul(rep[:], lhsT=ones[:], rhs=vec_rows[:, cols], start=True, stop=True)
+                nc.scalar.copy(out=bias_all[:, cols], in_=rep[:])
+            nc.vector.tensor_copy(out=gb_rows_f32[:], in_=gb_rows[:])
+            turned = turn_psum.tile([P, BANK], F32, tag="turn")
+            nc.tensor.transpose(turned[:, 0:P], gb_rows_f32[:], ident[:])
+            nc.scalar.copy(out=gb_cols[:], in_=turned[:, 0:2 * FEATURE_TILES])
 
         def quantised_tiles(name, width):
             codes = [keep.tile([P, width], U32, name="%s_codes%d" % (name, g), align_bytes=64)
@@ -99,9 +111,9 @@ def tile_gnnnicheencoder_pa_kernel(tc, h, W_l, b_l, W_r, ln_g, ln_b, out):
                       for g in range(PASSES)]
             return codes, scales
 
-        h_grouped = [keep.tile([P, ROWS, PACK], BF16, name="h_grouped%d" % g, align_bytes=64)
+        h_grouped = [keep.tile([P, RING_ROWS, PACK], BF16, name="h_grouped%d" % g, align_bytes=64)
                      for g in range(PASSES)]
-        m_grouped = [keep.tile([P, ROWS, PACK], BF16, name="m_grouped%d" % g, align_bytes=64)
+        m_grouped = [keep.tile([P, RING_ROWS, PACK], BF16, name="m_grouped%d" % g, align_bytes=64)
                      for g in range(PASSES)]
         h_codes, h_scales = quantised_tiles("h", ROWS)
         m_codes, m_scales = quantised_tiles("m", ROWS)
@@ -150,11 +162,17 @@ def tile_gnnnicheencoder_pa_kernel(tc, h, W_l, b_l, W_r, ln_g, ln_b, out):
             turned = turn_psum.tile([P, PACK, P], F32, tag="turn")
             for gu in range(PACK):
                 nc.tensor.transpose(turned[:, gu, :], words[:, gu * P:(gu + 1) * P], ident[:])
+            place = first % RING_ROWS
+            before_wrap = min(fresh, RING_ROWS - place)
+            pieces = [(0, place, before_wrap)]
+            if before_wrap < fresh:
+                pieces.append((before_wrap, 0, fresh - before_wrap))
             for g in range(PASSES):
-                nc.scalar.copy(
-                    out=h_grouped[g][:].bitcast(F32)[:, first:first + fresh, :],
-                    in_=turned[:, 2 * g:2 * g + 2, 0:fresh].rearrange("p u r -> p r u"),
-                )
+                for offset, at, count in pieces:
+                    nc.scalar.copy(
+                        out=h_grouped[g][:].bitcast(F32)[:, at:at + count, :],
+                        in_=turned[:, 2 * g:2 * g + 2, offset:offset + count].rearrange("p u r -> p r u"),
+                    )
 
             by_value = src[:].rearrange("p (g u q e) -> p g u e q", g=PASSES, u=2, e=2)
             for g in range(PASSES):
@@ -163,10 +181,11 @@ def tile_gnnnicheencoder_pa_kernel(tc, h, W_l, b_l, W_r, ln_g, ln_b, out):
                     for e in range(2):
                         nc.tensor.matmul(mean[:, 2 * u + e, :], lhsT=by_value[:, g, u, e, :], rhs=neigh[:],
                                          start=True, stop=True)
-                nc.scalar.copy(
-                    out=m_grouped[g][:, first:first + fresh, :],
-                    in_=mean[:, :, 0:fresh].rearrange("p t r -> p r t"),
-                )
+                for offset, at, count in pieces:
+                    nc.scalar.copy(
+                        out=m_grouped[g][:, at:at + count, :],
+                        in_=mean[:, :, offset:offset + count].rearrange("p t r -> p r t"),
+                    )
 
         def sources_for_rows_below(row):
             return -(-row // SRC_ROWS)
@@ -177,9 +196,10 @@ def tile_gnnnicheencoder_pa_kernel(tc, h, W_l, b_l, W_r, ln_g, ln_b, out):
 
         def quantise_rows(t):
             rows = slice(t * P, (t + 1) * P)
+            ring = slice((t % RING_TILES) * P, (t % RING_TILES + 1) * P)
             for g in range(PASSES):
-                quantise(h_grouped[g][:, rows, :], h_codes[g][:, rows], h_scales[g][:, rows])
-                quantise(m_grouped[g][:, rows, :], m_codes[g][:, rows], m_scales[g][:, rows])
+                quantise(h_grouped[g][:, ring, :], h_codes[g][:, rows], h_scales[g][:, rows])
+                quantise(m_grouped[g][:, ring, :], m_codes[g][:, rows], m_scales[g][:, rows])
 
         def multiply(t, half):
             rows = slice(t * P, (t + 1) * P)
@@ -204,12 +224,14 @@ def tile_gnnnicheencoder_pa_kernel(tc, h, W_l, b_l, W_r, ln_g, ln_b, out):
         c_sums = {}
         neg_means = {}
         rstds = {}
+        z_turned = {}
         y_tiles = {}
+        a_turned = {}
         h_tiles = {}
 
         def add_bias(t, half, acc):
             if half == 0:
-                c_tiles[t] = work.tile([P, D], F32, name="c", tag="c", bufs=LEAD + 2)
+                c_tiles[t] = work.tile([P, D], F32, name="c", tag="c", bufs=LEAD + 3)
                 c_sums[t] = stats.tile([P, HALVES], F32, name="c_sum", tag="c_sum")
             nc.vector.scalar_tensor_tensor(
                 out=c_tiles[t][:, halves[half]], in0=acc[:], scalar=1.0, in1=bias_all[:, halves[half]],
@@ -229,32 +251,52 @@ def tile_gnnnicheencoder_pa_kernel(tc, h, W_l, b_l, W_r, ln_g, ln_b, out):
             nc.scalar.activation(out=rstds[t][:], in_=sq_sum[:], func=ACT.Abs_reciprocal_sqrt, bias=eps[:, 0:1],
                                  scale=1.0 / D)
 
-        def centre_and_gain(t):
-            y_tiles[t] = work.tile([P, D], F32, name="y", tag="y")
-            nc.vector.scalar_tensor_tensor(
-                out=y_tiles[t][:], in0=c_tiles[t][:], scalar=neg_means[t][:, 0:1], in1=gain_all,
+        def normalise(t):
+            nc.vector.tensor_scalar(
+                out=c_tiles[t][:], in0=c_tiles[t][:], scalar1=neg_means[t][:, 0:1], scalar2=rstds[t][:, 0:1],
                 op0=ALU.add, op1=ALU.mult,
             )
 
-        def scale_and_shift(t):
-            nc.vector.scalar_tensor_tensor(
-                out=y_tiles[t][:], in0=y_tiles[t][:], scalar=rstds[t][:, 0:1], in1=shift_all,
-                op0=ALU.mult, op1=ALU.add,
-            )
+        def features_to_partitions(t):
+            z_turned[t] = []
+            for half in range(HALVES):
+                bank = turn_psum.tile([P, TILES_PER_BANK, P], F32, name="z_turned", tag="turn")
+                for i in range(TILES_PER_BANK):
+                    j = half * TILES_PER_BANK + i
+                    nc.tensor.transpose(bank[:, i, :], c_tiles[t][:, j * P:(j + 1) * P], ident[:])
+                z_turned[t].append(bank)
+
+        def gain_and_shift(t):
+            y_tiles[t] = work.tile([P, FEATURE_TILES, P], F32, name="y", tag="y")
+            for j in range(FEATURE_TILES):
+                nc.scalar.activation(
+                    out=y_tiles[t][:, j, :], in_=z_turned[t][j // TILES_PER_BANK][:, j % TILES_PER_BANK, :],
+                    func=ACT.Identity, scale=gain_col[:, j:j + 1], bias=shift_col[:, j:j + 1],
+                )
 
         def leaky_relu(t):
-            nc.vector.scalar_tensor_tensor(
-                out=y_tiles[t][:], in0=y_tiles[t][:], scalar=LEAKY_SLOPE, in1=y_tiles[t][:],
-                op0=ALU.mult, op1=ALU.max,
-            )
+            flat = y_tiles[t][:].rearrange("p j r -> p (j r)")
+            nc.vector.scalar_tensor_tensor(out=flat, in0=flat, scalar=LEAKY_SLOPE, in1=flat, op0=ALU.mult, op1=ALU.max)
+
+        def rows_to_partitions(t):
+            a_turned[t] = []
+            for half in range(HALVES):
+                bank = turn_psum.tile([P, BANK], F32, name="a_turned", tag="turn")
+                for i in range(TILES_PER_BANK):
+                    j = half * TILES_PER_BANK + i
+                    nc.tensor.transpose(bank[:, i * P:(i + 1) * P], y_tiles[t][:, j, :], ident[:])
+                a_turned[t].append(bank)
 
         def load_residual(t):
-            h_tiles[t] = work.tile([P, D], BF16, name="h_res", tag="h_res")
+            h_tiles[t] = work.tile([P, D], BF16, name="h_res", tag="h_res", bufs=4)
             nc.sync.dma_start(out=h_tiles[t][:], in_=h_rows[t * P:(t + 1) * P, :])
 
         def add_residual_and_store(t):
-            nc.vector.tensor_tensor(out=y_tiles[t][:], in0=y_tiles[t][:], in1=h_tiles[t][:], op=ALU.add)
-            nc.sync.dma_start(out=out_rows[t * P:(t + 1) * P, :], in_=y_tiles[t][:])
+            result = work.tile([P, D], F32, tag="result")
+            for half in range(HALVES):
+                nc.vector.tensor_tensor(out=result[:, halves[half]], in0=a_turned[t][half][:],
+                                        in1=h_tiles[t][:, halves[half]], op=ALU.add)
+            nc.sync.dma_start(out=out_rows[t * P:(t + 1) * P, :], in_=result[:])
 
         def is_tile(t):
             return 0 <= t < ROW_TILES
@@ -271,22 +313,25 @@ def tile_gnnnicheencoder_pa_kernel(tc, h, W_l, b_l, W_r, ln_g, ln_b, out):
         turn_rows(LEAD + 1)
         load_residual(0)
 
-        for t in range(ROW_TILES + 1):
+        for t in range(ROW_TILES + 2):
             if is_tile(t):
                 add_bias(t, 1, multiply(t, 1))
                 statistics(t)
-            if is_tile(t - 1):
-                scale_and_shift(t - 1)
             if is_tile(t + LEAD):
                 add_bias(t + LEAD, 0, multiply(t + LEAD, 0))
             if is_tile(t - 1):
-                leaky_relu(t - 1)
+                features_to_partitions(t - 1)
+                gain_and_shift(t - 1)
+            if is_tile(t - 2):
+                rows_to_partitions(t - 2)
             if is_tile(t + LEAD + 1):
                 quantise_rows(t + LEAD + 1)
-            if is_tile(t - 1):
-                add_residual_and_store(t - 1)
+            if is_tile(t - 2):
+                add_residual_and_store(t - 2)
             if is_tile(t):
-                centre_and_gain(t)
+                normalise(t)
+            if is_tile(t - 1):
+                leaky_relu(t - 1)
             if is_tile(t + LEAD + 2):
                 turn_rows(t + LEAD + 2)
             if is_tile(t + 1):

@@ -30,7 +30,7 @@ LEAD = 2
 FEATURE_TILES = D // P
 TILES_PER_BANK = BANK // P
 RING_TILES = 5
-RING_ROWS = RING_TILES * P
+OPERANDS = 2 * PASSES
 LN_EPS = 1e-5
 LEAKY_SLOPE = 0.01
 
@@ -111,12 +111,10 @@ def tile_gnnnicheencoder_pa_kernel(tc, h, W_l, b_l, W_r, ln_g, ln_b, out):
                       for g in range(PASSES)]
             return codes, scales
 
-        h_grouped = [keep.tile([P, RING_ROWS, PACK], BF16, name="h_grouped%d" % g, align_bytes=64)
-                     for g in range(PASSES)]
-        m_grouped = [keep.tile([P, RING_ROWS, PACK], BF16, name="m_grouped%d" % g, align_bytes=64)
-                     for g in range(PASSES)]
-        h_codes, h_scales = quantised_tiles("h", ROWS)
-        m_codes, m_scales = quantised_tiles("m", ROWS)
+        grouped = keep.tile([P, RING_TILES, OPERANDS, P, PACK], BF16, align_bytes=64)
+        grouped_words = grouped[:].bitcast(F32)
+        row_codes = keep.tile([P, ROW_TILES, OPERANDS, P], U32, align_bytes=64)
+        row_scales = keep.tile([P, ROW_TILES, OPERANDS, P], U8, align_bytes=64)
         wl_codes, wl_scales = quantised_tiles("wl", D)
         wr_codes, wr_scales = quantised_tiles("wr", D)
 
@@ -162,30 +160,29 @@ def tile_gnnnicheencoder_pa_kernel(tc, h, W_l, b_l, W_r, ln_g, ln_b, out):
             turned = turn_psum.tile([P, PACK, P], F32, tag="turn")
             for gu in range(PACK):
                 nc.tensor.transpose(turned[:, gu, :], words[:, gu * P:(gu + 1) * P], ident[:])
-            place = first % RING_ROWS
-            before_wrap = min(fresh, RING_ROWS - place)
-            pieces = [(0, place, before_wrap)]
-            if before_wrap < fresh:
-                pieces.append((before_wrap, 0, fresh - before_wrap))
-            for g in range(PASSES):
-                for offset, at, count in pieces:
-                    nc.scalar.copy(
-                        out=h_grouped[g][:].bitcast(F32)[:, at:at + count, :],
-                        in_=turned[:, 2 * g:2 * g + 2, offset:offset + count].rearrange("p u r -> p r u"),
-                    )
+            pieces = []
+            for row_tile in range(first // P, (first + fresh - 1) // P + 1):
+                low = max(first, row_tile * P)
+                high = min(first + fresh, (row_tile + 1) * P)
+                pieces.append((low - first, row_tile % RING_TILES, low - row_tile * P, high - low))
+            for offset, slot, at, count in pieces:
+                nc.scalar.copy(
+                    out=grouped_words[:, slot, 0:PASSES, at:at + count, :],
+                    in_=turned[:, :, offset:offset + count].rearrange("p (g u) r -> p g r u", u=2),
+                )
 
             by_value = src[:].rearrange("p (g u q e) -> p g u e q", g=PASSES, u=2, e=2)
+            mean = turn_psum.tile([P, PASSES, PACK, P], BF16, tag="turn")
             for g in range(PASSES):
-                mean = turn_psum.tile([P, PACK, P], F32, tag="turn")
                 for u in range(2):
                     for e in range(2):
-                        nc.tensor.matmul(mean[:, 2 * u + e, :], lhsT=by_value[:, g, u, e, :], rhs=neigh[:],
+                        nc.tensor.matmul(mean[:, g, 2 * u + e, :], lhsT=by_value[:, g, u, e, :], rhs=neigh[:],
                                          start=True, stop=True)
-                for offset, at, count in pieces:
-                    nc.scalar.copy(
-                        out=m_grouped[g][:, at:at + count, :],
-                        in_=mean[:, :, offset:offset + count].rearrange("p t r -> p r t"),
-                    )
+            for offset, slot, at, count in pieces:
+                nc.scalar.copy(
+                    out=grouped[:, slot, PASSES:OPERANDS, at:at + count, :],
+                    in_=mean[:, :, :, offset:offset + count].rearrange("p g v r -> p g r v"),
+                )
 
         def sources_for_rows_below(row):
             return -(-row // SRC_ROWS)
@@ -195,24 +192,23 @@ def tile_gnnnicheencoder_pa_kernel(tc, h, W_l, b_l, W_r, ln_g, ln_b, out):
                 turn_source(s)
 
         def quantise_rows(t):
-            rows = slice(t * P, (t + 1) * P)
-            ring = slice((t % RING_TILES) * P, (t % RING_TILES + 1) * P)
-            for g in range(PASSES):
-                quantise(h_grouped[g][:, ring, :], h_codes[g][:, rows], h_scales[g][:, rows])
-                quantise(m_grouped[g][:, ring, :], m_codes[g][:, rows], m_scales[g][:, rows])
+            nc.vector.quantize_mx(
+                out=row_codes[:, t].rearrange("p q r -> p (q r)").bitcast(FP8X4),
+                scales=row_scales[:, t].rearrange("p q r -> p (q r)"),
+                in_=grouped[:, t % RING_TILES].rearrange("p q r v -> p (q r v)"),
+            )
 
         def multiply(t, half):
-            rows = slice(t * P, (t + 1) * P)
             products = []
             for g in range(PASSES):
-                products.append((m_codes[g], m_scales[g], wl_codes[g], wl_scales[g]))
-                products.append((h_codes[g], h_scales[g], wr_codes[g], wr_scales[g]))
+                products.append((PASSES + g, wl_codes[g], wl_scales[g]))
+                products.append((g, wr_codes[g], wr_scales[g]))
             acc = acc_psum.tile([P, BANK], F32, tag="acc")
-            for i, (x_codes, x_scales, w_codes, w_scales) in enumerate(products):
+            for i, (q, w_codes, w_scales) in enumerate(products):
                 nc.tensor.matmul_mx(
                     out=acc[:],
-                    lhsT=x_codes[:, rows].bitcast(FP8X4),
-                    lhsT_scale=x_scales[:, rows],
+                    lhsT=row_codes[:, t, q, :].bitcast(FP8X4),
+                    lhsT_scale=row_scales[:, t, q, :],
                     rhs=w_codes[:, halves[half]].bitcast(FP8X4),
                     rhs_scale=w_scales[:, halves[half]],
                     start=(i == 0),

@@ -29,6 +29,10 @@ SRC_ROWS = SRC_GRAPHS * NODES
 LEAD = 2
 FEATURE_TILES = D // P
 TILES_PER_BANK = BANK // P
+DIRECT_TILES = 2
+TURNED_TILES = FEATURE_TILES - DIRECT_TILES
+TURNED = TURNED_TILES * P
+DIRECT = DIRECT_TILES * P
 RING_TILES = 5
 OPERANDS = 2 * PASSES
 LN_EPS = 1e-5
@@ -90,6 +94,11 @@ def tile_gnnnicheencoder_pa_kernel(tc, h, W_l, b_l, W_r, ln_g, ln_b, out):
         nc.vector.memset(gb_rows[:], 0.0)
         nc.scalar.dma_start(out=gb_rows[0:FEATURE_TILES, :], in_=ln_g.rearrange("(j p) -> j p", p=P))
         nc.scalar.dma_start(out=gb_rows[FEATURE_TILES:2 * FEATURE_TILES, :], in_=ln_b.rearrange("(j p) -> j p", p=P))
+        direct_rows = consts.tile([P, 2, DIRECT], BF16)
+        nc.vector.memset(direct_rows[:], 0.0)
+        nc.scalar.dma_start(out=direct_rows[0:1, 0, :], in_=ln_g[TURNED:D].unsqueeze(0))
+        nc.scalar.dma_start(out=direct_rows[0:1, 1, :], in_=ln_b[TURNED:D].unsqueeze(0))
+        direct_all = consts.tile([P, 2, DIRECT], BF16)
         gb_rows_f32 = consts.tile([P, P], F32)
         gb_cols = consts.tile([P, 2 * FEATURE_TILES], F32)
         gain_col, shift_col = gb_cols[:, 0:FEATURE_TILES], gb_cols[:, FEATURE_TILES:2 * FEATURE_TILES]
@@ -99,6 +108,10 @@ def tile_gnnnicheencoder_pa_kernel(tc, h, W_l, b_l, W_r, ln_g, ln_b, out):
                 rep = turn_psum.tile([P, BANK], F32, tag="turn")
                 nc.tensor.matmul(rep[:], lhsT=ones[:], rhs=vec_rows[:, cols], start=True, stop=True)
                 nc.scalar.copy(out=bias_all[:, cols], in_=rep[:])
+            rep = turn_psum.tile([P, BANK], F32, tag="turn")
+            nc.tensor.matmul(rep[:, 0:2 * DIRECT], lhsT=ones[:], rhs=direct_rows[:].rearrange("p v c -> p (v c)"),
+                             start=True, stop=True)
+            nc.scalar.copy(out=direct_all[:].rearrange("p v c -> p (v c)"), in_=rep[:, 0:2 * DIRECT])
             nc.vector.tensor_copy(out=gb_rows_f32[:], in_=gb_rows[:])
             turned = turn_psum.tile([P, BANK], F32, tag="turn")
             nc.tensor.transpose(turned[:, 0:P], gb_rows_f32[:], ident[:])
@@ -249,22 +262,30 @@ def tile_gnnnicheencoder_pa_kernel(tc, h, W_l, b_l, W_r, ln_g, ln_b, out):
 
         def normalise(t):
             nc.vector.tensor_scalar(
-                out=c_tiles[t][:], in0=c_tiles[t][:], scalar1=neg_means[t][:, 0:1], scalar2=rstds[t][:, 0:1],
+                out=c_tiles[t][:, 0:TURNED], in0=c_tiles[t][:, 0:TURNED], scalar1=neg_means[t][:, 0:1],
+                scalar2=rstds[t][:, 0:1], op0=ALU.add, op1=ALU.mult,
+            )
+            y_tiles[t] = work.tile([P, FEATURE_TILES, P], F32, name="y", tag="y", bufs=4)
+            y_direct = y_tiles[t][:, TURNED_TILES:FEATURE_TILES, :].rearrange("p j r -> p (j r)")
+            nc.vector.scalar_tensor_tensor(
+                out=y_direct, in0=c_tiles[t][:, TURNED:D], scalar=neg_means[t][:, 0:1], in1=direct_all[:, 0, :],
                 op0=ALU.add, op1=ALU.mult,
+            )
+            nc.vector.scalar_tensor_tensor(
+                out=y_direct, in0=y_direct, scalar=rstds[t][:, 0:1], in1=direct_all[:, 1, :],
+                op0=ALU.mult, op1=ALU.add,
             )
 
         def features_to_partitions(t):
             z_turned[t] = []
             for half in range(HALVES):
                 bank = turn_psum.tile([P, TILES_PER_BANK, P], F32, name="z_turned", tag="turn")
-                for i in range(TILES_PER_BANK):
-                    j = half * TILES_PER_BANK + i
-                    nc.tensor.transpose(bank[:, i, :], c_tiles[t][:, j * P:(j + 1) * P], ident[:])
+                for j in range(half * TILES_PER_BANK, min((half + 1) * TILES_PER_BANK, TURNED_TILES)):
+                    nc.tensor.transpose(bank[:, j % TILES_PER_BANK, :], c_tiles[t][:, j * P:(j + 1) * P], ident[:])
                 z_turned[t].append(bank)
 
         def gain_and_shift(t):
-            y_tiles[t] = work.tile([P, FEATURE_TILES, P], F32, name="y", tag="y")
-            for j in range(FEATURE_TILES):
+            for j in range(TURNED_TILES):
                 nc.scalar.activation(
                     out=y_tiles[t][:, j, :], in_=z_turned[t][j // TILES_PER_BANK][:, j % TILES_PER_BANK, :],
                     func=ACT.Identity, scale=gain_col[:, j:j + 1], bias=shift_col[:, j:j + 1],
@@ -278,8 +299,8 @@ def tile_gnnnicheencoder_pa_kernel(tc, h, W_l, b_l, W_r, ln_g, ln_b, out):
             a_turned[t] = []
             for half in range(HALVES):
                 bank = turn_psum.tile([P, BANK], F32, name="a_turned", tag="turn")
-                for i in range(TILES_PER_BANK):
-                    j = half * TILES_PER_BANK + i
+                for j in range(half * TILES_PER_BANK, min((half + 1) * TILES_PER_BANK, TURNED_TILES)):
+                    i = j % TILES_PER_BANK
                     nc.tensor.transpose(bank[:, i * P:(i + 1) * P], y_tiles[t][:, j, :], ident[:])
                 a_turned[t].append(bank)
 
@@ -290,8 +311,12 @@ def tile_gnnnicheencoder_pa_kernel(tc, h, W_l, b_l, W_r, ln_g, ln_b, out):
         def add_residual_and_store(t):
             result = work.tile([P, D], F32, tag="result")
             for half in range(HALVES):
-                nc.vector.tensor_tensor(out=result[:, halves[half]], in0=a_turned[t][half][:],
-                                        in1=h_tiles[t][:, halves[half]], op=ALU.add)
+                cols = slice(half * BANK, min((half + 1) * BANK, TURNED))
+                nc.vector.tensor_tensor(out=result[:, cols], in0=a_turned[t][half][:, 0:cols.stop - cols.start],
+                                        in1=h_tiles[t][:, cols], op=ALU.add)
+            nc.vector.tensor_tensor(
+                out=result[:, TURNED:D], in0=y_tiles[t][:, TURNED_TILES:FEATURE_TILES, :].rearrange("p j r -> p (j r)"),
+                in1=h_tiles[t][:, TURNED:D], op=ALU.add)
             nc.sync.dma_start(out=out_rows[t * P:(t + 1) * P, :], in_=result[:])
 
         def is_tile(t):

@@ -261,15 +261,15 @@ def tile_gnnnicheencoder_pa_kernel(tc, h, W_l, b_l, W_r, ln_g, ln_b, out):
                                  scale=1.0 / D)
 
         def normalise(t):
-            nc.vector.tensor_scalar(
-                out=c_tiles[t][:, 0:TURNED], in0=c_tiles[t][:, 0:TURNED], scalar1=neg_means[t][:, 0:1],
-                scalar2=rstds[t][:, 0:1], op0=ALU.add, op1=ALU.mult,
-            )
             y_tiles[t] = work.tile([P, FEATURE_TILES, P], F32, name="y", tag="y", bufs=4)
             y_direct = y_tiles[t][:, TURNED_TILES:FEATURE_TILES, :].rearrange("p j r -> p (j r)")
             nc.vector.scalar_tensor_tensor(
                 out=y_direct, in0=c_tiles[t][:, TURNED:D], scalar=neg_means[t][:, 0:1], in1=direct_all[:, 0, :],
                 op0=ALU.add, op1=ALU.mult,
+            )
+            nc.vector.tensor_scalar(
+                out=c_tiles[t][:, 0:TURNED], in0=c_tiles[t][:, 0:TURNED], scalar1=neg_means[t][:, 0:1],
+                scalar2=rstds[t][:, 0:1], op0=ALU.add, op1=ALU.mult,
             )
             nc.vector.scalar_tensor_tensor(
                 out=y_direct, in0=y_direct, scalar=rstds[t][:, 0:1], in1=direct_all[:, 1, :],

from contextlib import ExitStack

import concourse.mybir as mybir
from concourse.masks import make_identity

F32 = mybir.dt.float32
BF16 = mybir.dt.bfloat16
U32 = mybir.dt.uint32
U8 = mybir.dt.uint8
FP8X4 = mybir.dt.float8_e4m3fn_x4
ALU = mybir.AluOpType
ACT = mybir.ActivationFunctionType

P = 128
GRAPHS = 128
NODES = 17
ROWS = GRAPHS * NODES
D = 1024
PACK = 4
K_PASS = P * PACK
PASSES = D // K_PASS
BANK = 512
HALVES = D // BANK
ROW_TILES = ROWS // P
W_TILES_PER_LOAD = 2
W_LOADS_PER_HALF = BANK // (P * W_TILES_PER_LOAD)
SRC_GRAPHS = P // NODES
SRC_ROWS = SRC_GRAPHS * NODES
LEAD = 2
FEATURE_TILES = D // P
TILES_PER_BANK = BANK // P
DIRECT_TILES = 2
TURNED_TILES = FEATURE_TILES - DIRECT_TILES
TURNED = TURNED_TILES * P
DIRECT = DIRECT_TILES * P
RING_TILES = 5
OPERANDS = 2 * PASSES
LN_EPS = 1e-5
LEAKY_SLOPE = 0.01

FLOPS = 2 * 2 * ROWS * D * D


def tile_gnnnicheencoder_pa_kernel(tc, h, W_l, b_l, W_r, ln_g, ln_b, out):
    nc = tc.nc
    h_rows = h.flatten_outer_dims()
    out_rows = out.flatten_outer_dims()
    halves = [slice(half * BANK, (half + 1) * BANK) for half in range(HALVES)]

    with ExitStack() as stack:
        consts = stack.enter_context(tc.tile_pool(name="consts", bufs=1))
        keep = stack.enter_context(tc.tile_pool(name="keep", bufs=1))
        w_stage = stack.enter_context(tc.tile_pool(name="w_stage", bufs=4))
        src_pool = stack.enter_context(tc.tile_pool(name="src", bufs=5))
        work = stack.enter_context(tc.tile_pool(name="work", bufs=3))
        stats = stack.enter_context(tc.tile_pool(name="stats", bufs=LEAD + 3))
        turn_psum = stack.enter_context(tc.psum_pool(name="turn_psum", bufs=6))
        acc_psum = stack.enter_context(tc.psum_pool(name="acc_psum", bufs=2))

        eps = consts.tile([P, 1], F32)
        nc.vector.memset(eps[:], LN_EPS)
        warm = consts.tile([P, 1], F32)
        nc.scalar.activation(out=warm[:], in_=eps[:], func=ACT.Abs_reciprocal_sqrt)

        ident = consts.tile([P, P], F32)
        make_identity(nc, ident[:])

        neigh_f32 = consts.tile([P, P], F32)
        nc.gpsimd.memset(neigh_f32[:], 0.0)
        nc.gpsimd.memset(neigh_f32[:, 0:SRC_ROWS], 1.0 / (NODES - 1))
        by_graph = neigh_f32[:, 0:SRC_ROWS].rearrange("p (c j) -> p c j", j=NODES)
        nc.gpsimd.affine_select(
            out=by_graph, in_=by_graph, compare_op=ALU.is_ge, fill=0.0,
            base=0, pattern=[[-NODES, SRC_GRAPHS], [0, NODES]], channel_multiplier=1,
        )
        nc.gpsimd.affine_select(
            out=by_graph, in_=by_graph, compare_op=ALU.is_ge, fill=0.0,
            base=NODES - 1, pattern=[[NODES, SRC_GRAPHS], [0, NODES]], channel_multiplier=-1,
        )
        nc.gpsimd.affine_select(
            out=neigh_f32[:], in_=neigh_f32[:], compare_op=ALU.not_equal, fill=0.0,
            base=0, pattern=[[-1, P]], channel_multiplier=1,
        )
        neigh = consts.tile([P, P], BF16)
        nc.vector.tensor_copy(out=neigh[:], in_=neigh_f32[:])

        ones = consts.tile([P, P], BF16)
        nc.vector.memset(ones[:], 1.0)
        vec_rows = consts.tile([P, D], BF16)
        nc.vector.memset(vec_rows[:], 0.0)
        nc.scalar.dma_start(out=vec_rows[0:1, :], in_=b_l.unsqueeze(0))
        bias_all = consts.tile([P, D], BF16)
        gb_rows = consts.tile([P, P], BF16)
        nc.vector.memset(gb_rows[:], 0.0)
        nc.scalar.dma_start(out=gb_rows[0:FEATURE_TILES, :], in_=ln_g.rearrange("(j p) -> j p", p=P))
        nc.scalar.dma_start(out=gb_rows[FEATURE_TILES:2 * FEATURE_TILES, :], in_=ln_b.rearrange("(j p) -> j p", p=P))
        direct_rows = consts.tile([P, 2, DIRECT], BF16)
        nc.vector.memset(direct_rows[:], 0.0)
        nc.scalar.dma_start(out=direct_rows[0:1, 0, :], in_=ln_g[TURNED:D].unsqueeze(0))
        nc.scalar.dma_start(out=direct_rows[0:1, 1, :], in_=ln_b[TURNED:D].unsqueeze(0))
        direct_all = consts.tile([P, 2, DIRECT], BF16)
        gb_rows_f32 = consts.tile([P, P], F32)
        gb_cols = consts.tile([P, 2 * FEATURE_TILES], F32)
        gain_col, shift_col = gb_cols[:, 0:FEATURE_TILES], gb_cols[:, FEATURE_TILES:2 * FEATURE_TILES]

        def spread_vectors():
            for cols in halves:
                rep = turn_psum.tile([P, BANK], F32, tag="turn")
                nc.tensor.matmul(rep[:], lhsT=ones[:], rhs=vec_rows[:, cols], start=True, stop=True)
                nc.scalar.copy(out=bias_all[:, cols], in_=rep[:])
            rep = turn_psum.tile([P, BANK], F32, tag="turn")
            nc.tensor.matmul(rep[:, 0:2 * DIRECT], lhsT=ones[:], rhs=direct_rows[:].rearrange("p v c -> p (v c)"),
                             start=True, stop=True)
            nc.scalar.copy(out=direct_all[:].rearrange("p v c -> p (v c)"), in_=rep[:, 0:2 * DIRECT])
            nc.vector.tensor_copy(out=gb_rows_f32[:], in_=gb_rows[:])
            turned = turn_psum.tile([P, BANK], F32, tag="turn")
            nc.tensor.transpose(turned[:, 0:P], gb_rows_f32[:], ident[:])
            nc.scalar.copy(out=gb_cols[:], in_=turned[:, 0:2 * FEATURE_TILES])

        def quantised_tiles(name, width):
            codes = [keep.tile([P, width], U32, name="%s_codes%d" % (name, g), align_bytes=64)
                     for g in range(PASSES)]
            scales = [keep.tile([P, width], U8, name="%s_scales%d" % (name, g), align_bytes=64)
                      for g in range(PASSES)]
            return codes, scales

        grouped = keep.tile([P, RING_TILES, OPERANDS, P, PACK], BF16, align_bytes=64)
        grouped_words = grouped[:].bitcast(F32)
        row_codes = keep.tile([P, ROW_TILES, OPERANDS, P], U32, align_bytes=64)
        row_scales = keep.tile([P, ROW_TILES, OPERANDS, P], U8, align_bytes=64)
        wl_codes, wl_scales = quantised_tiles("wl", D)
        wr_codes, wr_scales = quantised_tiles("wr", D)

        def quantise(grouped, codes, scales):
            nc.vector.quantize_mx(
                out=codes.bitcast(FP8X4), scales=scales, in_=grouped.rearrange("p c t -> p (c t)"))

        def prepare_weights(half):
            for w, codes, scales in ((W_l, wl_codes, wl_scales), (W_r, wr_codes, wr_scales)):
                by_tile = w.rearrange("(t p) k -> p t k", p=P)
                w_grouped = [w_stage.tile([P, BANK, PACK], BF16, name="w_grouped%d" % g, tag="w_grouped",
                                          align_bytes=64) for g in range(PASSES)]
                for load in range(W_LOADS_PER_HALF):
                    first_tile = (half * W_LOADS_PER_HALF + load) * W_TILES_PER_LOAD
                    w_nat = w_stage.tile([P, W_TILES_PER_LOAD, D], BF16, tag="w_nat")
                    nc.sync.dma_start(out=w_nat[:], in_=by_tile[:, first_tile:first_tile + W_TILES_PER_LOAD, :])
                    for i in range(W_TILES_PER_LOAD):
                        words = w_nat[:, i, :].bitcast(F32)
                        turned = turn_psum.tile([P, PACK, P], F32, tag="turn")
                        for gu in range(PACK):
                            nc.tensor.transpose(turned[:, gu, :], words[:, gu * P:(gu + 1) * P], ident[:])
                        first_col = (load * W_TILES_PER_LOAD + i) * P
                        for g in range(PASSES):
                            dst = w_grouped[g][:].bitcast(F32)[:, first_col:first_col + P, :]
                            pairs = turned[:, 2 * g:2 * g + 2, :].rearrange("p u o -> p o u")
                            if i % 2 == 0:
                                nc.scalar.copy(out=dst, in_=pairs)
                            else:
                                nc.vector.tensor_copy(out=dst, in_=pairs)
                for g in range(PASSES):
                    quantise(w_grouped[g][:], codes[g][:, halves[half]], scales[g][:, halves[half]])

        def turn_source(s):
            first = s * SRC_ROWS
            fresh = min(SRC_ROWS, ROWS - first)
            loaded = min(P, ROWS - first)
            src = src_pool.tile([P, D], BF16)
            if loaded < P:
                nc.gpsimd.memset(src[:], 0.0)
            nc.sync.dma_start(out=src[0:loaded, :], in_=h_rows[first:first + loaded, :])

            words = src[:].bitcast(F32)
            turned = turn_psum.tile([P, PACK, P], F32, tag="turn")
            for gu in range(PACK):
                nc.tensor.transpose(turned[:, gu, :], words[:, gu * P:(gu + 1) * P], ident[:])
            pieces = []
            for row_tile in range(first // P, (first + fresh - 1) // P + 1):
                low = max(first, row_tile * P)
                high = min(first + fresh, (row_tile + 1) * P)
                pieces.append((low - first, row_tile % RING_TILES, low - row_tile * P, high - low))
            for offset, slot, at, count in pieces:
                nc.scalar.copy(
                    out=grouped_words[:, slot, 0:PASSES, at:at + count, :],
                    in_=turned[:, :, offset:offset + count].rearrange("p (g u) r -> p g r u", u=2),
                )

            by_value = src[:].rearrange("p (g u q e) -> p g u e q", g=PASSES, u=2, e=2)
            mean = turn_psum.tile([P, PASSES, PACK, P], BF16, tag="turn")
            for g in range(PASSES):
                for u in range(2):
                    for e in range(2):
                        nc.tensor.matmul(mean[:, g, 2 * u + e, :], lhsT=by_value[:, g, u, e, :], rhs=neigh[:],
                                         start=True, stop=True)
            for offset, slot, at, count in pieces:
                nc.scalar.copy(
                    out=grouped[:, slot, PASSES:OPERANDS, at:at + count, :],
                    in_=mean[:, :, :, offset:offset + count].rearrange("p g v r -> p g r v"),
                )

        def sources_for_rows_below(row):
            return -(-row // SRC_ROWS)

        def turn_rows(t):
            for s in range(sources_for_rows_below(t * P), sources_for_rows_below((t + 1) * P)):
                turn_source(s)

        def quantise_rows(t):
            nc.vector.quantize_mx(
                out=row_codes[:, t].rearrange("p q r -> p (q r)").bitcast(FP8X4),
                scales=row_scales[:, t].rearrange("p q r -> p (q r)"),
                in_=grouped[:, t % RING_TILES].rearrange("p q r v -> p (q r v)"),
            )

        def multiply(t, half):
            products = []
            for g in range(PASSES):
                products.append((PASSES + g, wl_codes[g], wl_scales[g]))
                products.append((g, wr_codes[g], wr_scales[g]))
            acc = acc_psum.tile([P, BANK], F32, tag="acc")
            for i, (q, w_codes, w_scales) in enumerate(products):
                nc.tensor.matmul_mx(
                    out=acc[:],
                    lhsT=row_codes[:, t, q, :].bitcast(FP8X4),
                    lhsT_scale=row_scales[:, t, q, :],
                    rhs=w_codes[:, halves[half]].bitcast(FP8X4),
                    rhs_scale=w_scales[:, halves[half]],
                    start=(i == 0),
                    stop=(i == len(products) - 1),
                )
            return acc

        c_tiles = {}
        c_sums = {}
        neg_means = {}
        rstds = {}
        z_turned = {}
        y_tiles = {}
        a_turned = {}
        h_tiles = {}

        def add_bias(t, half, acc):
            if half == 0:
                c_tiles[t] = work.tile([P, D], F32, name="c", tag="c", bufs=LEAD + 3)
                c_sums[t] = stats.tile([P, HALVES], F32, name="c_sum", tag="c_sum")
            nc.vector.scalar_tensor_tensor(
                out=c_tiles[t][:, halves[half]], in0=acc[:], scalar=1.0, in1=bias_all[:, halves[half]],
                op0=ALU.mult, op1=ALU.add, accum_out=c_sums[t][:, half:half + 1],
            )

        def statistics(t):
            scaled = stats.tile([P, HALVES], F32, tag="scaled")
            neg_means[t] = stats.tile([P, 1], F32, name="neg_mean", tag="neg_mean")
            nc.scalar.activation(out=scaled[:], in_=c_sums[t][:], func=ACT.Identity, scale=-1.0 / D,
                                 accum_out=neg_means[t][:])
            squares = work.tile([P, D], BF16, tag="squares", bufs=2)
            sq_sum = stats.tile([P, 1], F32, tag="sq_sum")
            nc.scalar.activation(out=squares[:], in_=c_tiles[t][:], func=ACT.Square, bias=neg_means[t][:, 0:1],
                                 scale=1.0, accum_out=sq_sum[:])
            rstds[t] = stats.tile([P, 1], F32, name="rstd", tag="rstd")
            nc.scalar.activation(out=rstds[t][:], in_=sq_sum[:], func=ACT.Abs_reciprocal_sqrt, bias=eps[:, 0:1],
                                 scale=1.0 / D)

        def normalise(t):
            y_tiles[t] = work.tile([P, FEATURE_TILES, P], F32, name="y", tag="y", bufs=4)
            y_direct = y_tiles[t][:, TURNED_TILES:FEATURE_TILES, :].rearrange("p j r -> p (j r)")
            nc.vector.scalar_tensor_tensor(
                out=y_direct, in0=c_tiles[t][:, TURNED:D], scalar=neg_means[t][:, 0:1], in1=direct_all[:, 0, :],
                op0=ALU.add, op1=ALU.mult,
            )
            nc.vector.tensor_scalar(
                out=c_tiles[t][:, 0:TURNED], in0=c_tiles[t][:, 0:TURNED], scalar1=neg_means[t][:, 0:1],
                scalar2=rstds[t][:, 0:1], op0=ALU.add, op1=ALU.mult,
            )
            nc.vector.scalar_tensor_tensor(
                out=y_direct, in0=y_direct, scalar=rstds[t][:, 0:1], in1=direct_all[:, 1, :],
                op0=ALU.mult, op1=ALU.add,
            )

        def features_to_partitions(t):
            z_turned[t] = []
            for half in range(HALVES):
                bank = turn_psum.tile([P, TILES_PER_BANK, P], F32, name="z_turned", tag="turn")
                for j in range(half * TILES_PER_BANK, min((half + 1) * TILES_PER_BANK, TURNED_TILES)):
                    nc.tensor.transpose(bank[:, j % TILES_PER_BANK, :], c_tiles[t][:, j * P:(j + 1) * P], ident[:])
                z_turned[t].append(bank)

        def gain_and_shift(t):
            for j in range(TURNED_TILES):
                nc.scalar.activation(
                    out=y_tiles[t][:, j, :], in_=z_turned[t][j // TILES_PER_BANK][:, j % TILES_PER_BANK, :],
                    func=ACT.Identity, scale=gain_col[:, j:j + 1], bias=shift_col[:, j:j + 1],
                )

        def leaky_relu(t):
            flat = y_tiles[t][:].rearrange("p j r -> p (j r)")
            nc.vector.scalar_tensor_tensor(out=flat, in0=flat, scalar=LEAKY_SLOPE, in1=flat, op0=ALU.mult, op1=ALU.max)

        def rows_to_partitions(t):
            a_turned[t] = []
            for half in range(HALVES):
                bank = turn_psum.tile([P, BANK], F32, name="a_turned", tag="turn")
                for j in range(half * TILES_PER_BANK, min((half + 1) * TILES_PER_BANK, TURNED_TILES)):
                    i = j % TILES_PER_BANK
                    nc.tensor.transpose(bank[:, i * P:(i + 1) * P], y_tiles[t][:, j, :], ident[:])
                a_turned[t].append(bank)

        def load_residual(t):
            h_tiles[t] = work.tile([P, D], BF16, name="h_res", tag="h_res", bufs=4)
            nc.sync.dma_start(out=h_tiles[t][:], in_=h_rows[t * P:(t + 1) * P, :])

        def add_residual_and_store(t):
            result = work.tile([P, D], F32, tag="result")
            for half in range(HALVES):
                cols = slice(half * BANK, min((half + 1) * BANK, TURNED))
                nc.vector.tensor_tensor(out=result[:, cols], in0=a_turned[t][half][:, 0:cols.stop - cols.start],
                                        in1=h_tiles[t][:, cols], op=ALU.add)
            nc.vector.tensor_tensor(
                out=result[:, TURNED:D], in0=y_tiles[t][:, TURNED_TILES:FEATURE_TILES, :].rearrange("p j r -> p (j r)"),
                in1=h_tiles[t][:, TURNED:D], op=ALU.add)
            nc.sync.dma_start(out=out_rows[t * P:(t + 1) * P, :], in_=result[:])

        def is_tile(t):
            return 0 <= t < ROW_TILES

        prepare_weights(0)
        for t in range(LEAD + 1):
            turn_rows(t)
        spread_vectors()
        for t in range(LEAD):
            quantise_rows(t)
            add_bias(t, 0, multiply(t, 0))
        quantise_rows(LEAD)
        prepare_weights(1)
        turn_rows(LEAD + 1)
        load_residual(0)

        for t in range(ROW_TILES + 2):
            if is_tile(t):
                add_bias(t, 1, multiply(t, 1))
                statistics(t)
            if is_tile(t + LEAD):
                add_bias(t + LEAD, 0, multiply(t + LEAD, 0))
            if is_tile(t - 1):
                features_to_partitions(t - 1)
                gain_and_shift(t - 1)
            if is_tile(t - 2):
                rows_to_partitions(t - 2)
            if is_tile(t + LEAD + 1):
                quantise_rows(t + LEAD + 1)
            if is_tile(t - 2):
                add_residual_and_store(t - 2)
            if is_tile(t):
                normalise(t)
            if is_tile(t - 1):
                leaky_relu(t - 1)
            if is_tile(t + LEAD + 2):
                turn_rows(t + LEAD + 2)
            if is_tile(t + 1):
                load_residual(t + 1)
